import numpy as np
import ml_dtypes


def mxq(x, axis, fmt="e4m3"):
    dtype, down = {"e4m3": (ml_dtypes.float8_e4m3fn, 7), "e5m2": (ml_dtypes.float8_e5m2, 14)}[fmt]
    v = np.moveaxis(np.asarray(x, np.float32).astype(ml_dtypes.bfloat16).astype(np.float64), axis, -1)
    blocks = v.reshape(v.shape[:-1] + (-1, 32))
    amax = np.abs(blocks).max(-1, keepdims=True)
    byte = np.maximum(np.where(amax > 0, np.frexp(amax)[1] - 1 + 127, 0) - down, 1)
    scale = np.exp2(byte - 127.0)
    codes = (blocks / scale).astype(np.float32).astype(dtype).astype(np.float64)
    return np.moveaxis((codes * scale).reshape(v.shape), -1, axis)


WIDE = False


def mx_kscale(k):
    if not WIDE:
        return np.ones(k)
    levels = np.array([10, -10, 5, -5, 0])
    a = np.random.permutation(np.resize(levels, k // 512 * 4)).reshape(k // 512, 4)
    idx = np.arange(k)
    return np.exp2(a[idx // 512, idx % 128 // 32])


BF16 = ml_dtypes.bfloat16


def bf(x):
    return np.asarray(x, np.float32).astype(BF16)


def f64(x):
    return np.asarray(x).astype(np.float64)


E2M1 = np.array([0.0, 0.5, 1.0, 1.5, 2.0, 3.0, 4.0, 6.0, -0.0, -0.5, -1.0, -1.5, -2.0, -3.0, -4.0, -6.0])


def pack_weight(w, fmt):
    k, n = w.shape
    w = f64(bf(w)).reshape(k // 32, 32, n)
    amax = np.abs(w).max(1)
    if fmt == "e4m3":
        byte = np.frexp(amax)[1] - 1 + 127 - 7
    else:
        mant, ex = np.frexp(amax / 6.0)
        byte = np.where(mant > 0.5, ex, ex - 1) + 127
    byte = np.clip(np.where(amax > 0, byte, 1), 1, 254)
    scaled = (w * np.exp2(127.0 - byte)[:, None, :]).reshape(k, n).astype(np.float32)
    by_word = np.ascontiguousarray(scaled.reshape(k // 512, 128, 4, n).transpose(0, 1, 3, 2))
    if fmt == "e4m3":
        words = by_word.astype(ml_dtypes.float8_e4m3fn).view(np.uint8)
    else:
        c = by_word.astype(ml_dtypes.float4_e2m1fn).view(np.uint8) & 0xF
        words = c[..., 0::2] | (c[..., 1::2] << 4)
    return np.ascontiguousarray(words), np.ascontiguousarray(byte.astype(np.uint8).reshape(k // 512, 16, n))


def unpack_weight(words, scales, fmt):
    g, p, n, _ = words.shape
    if fmt == "e4m3":
        vals = np.ascontiguousarray(words).view(ml_dtypes.float8_e4m3fn).astype(np.float64)
    else:
        nib = np.empty((g, p, n, 4), np.uint8)
        nib[..., 0::2] = words & 0xF
        nib[..., 1::2] = words >> 4
        vals = E2M1[nib]
    vals = vals * np.repeat(np.exp2(scales.astype(np.float64) - 127.0), 8, axis=1)[..., None]
    return vals.transpose(0, 1, 3, 2).reshape(g * 512, n)

def pack4(w):
    words, scales = pack_weight(w, "e2m1")
    return words.reshape(words.shape[0], 128, -1), scales


def unpack4(words, scales):
    return unpack_weight(words.reshape(words.shape[0], 128, -1, 2), scales, "e2m1")


B, T, C, H, D, R = 4, 1024, 1024, 8, 128, 512
EPS = 1e-6
THETA = 10000.0


def rmsnorm(v, w):
    var = np.mean(v * v, axis=-1, keepdims=True)
    return v * (1.0 / np.sqrt(var + EPS)) * w


def rope(v, cos, sin):
    re, im = v[..., 0::2], v[..., 1::2]
    c, s = cos[None, :, None, :], sin[None, :, None, :]
    return np.stack([re * c - im * s, re * s + im * c], axis=-1).reshape(v.shape)


def setup_inputs():
    s = mx_kscale(C)
    ang = np.outer(np.arange(T), 1.0 / THETA ** (np.arange(0, D, 2) / D))
    x = bf(np.random.standard_normal((B, T, C)) * s)
    wq = np.random.standard_normal((H * D, C)) / np.sqrt(C) / s[None, :]
    wq_words, wq_scales = pack4(np.ascontiguousarray(wq.T))
    q_norm_w = bf(1.0 + 0.1 * np.random.standard_normal(D))
    return {"x": x,
            "wq_words": wq_words, "wq_scales": wq_scales,
            "q_norm_w": q_norm_w,
            "freqs_cos": bf(np.cos(ang)), "freqs_sin": bf(np.sin(ang))}


def reference(x, wq_words, wq_scales, q_norm_w, freqs_cos, freqs_sin):
    xq = (mxq(f64(x), 2, "e4m3") @ unpack4(wq_words, wq_scales)).reshape(B, T, H, D)
    return rope(rmsnorm(xq, f64(q_norm_w)), f64(freqs_cos), f64(freqs_sin))

@@ -1,0 +1,194 @@
+from contextlib import ExitStack
+
+import concourse.mybir as mybir
+from concourse.masks import make_identity
+
+F32 = mybir.dt.float32
+BF16 = mybir.dt.bfloat16
+I32 = mybir.dt.int32
+U32 = mybir.dt.uint32
+U8 = mybir.dt.uint8
+FP8X4 = mybir.dt.float8_e4m3fn_x4
+FP4X4 = mybir.dt.float4_e2m1fn_x4
+ACT = mybir.ActivationFunctionType
+ALU = mybir.AluOpType
+
+P = 128
+TOKENS = 4 * 1024
+SEQ = 1024
+K = 1024
+K_PASS = 512
+PASSES = K // K_PASS
+WORDS = K_PASS // 2
+HEADS = 8
+HEAD = 128
+PAIRS = HEAD // 2
+BANK = 512
+BANKS = HEADS * HEAD // BANK
+BANK_HEADS = BANK // HEAD
+TILES_IN_BLOCK = 4
+BLOCK = TILES_IN_BLOCK * P
+BLOCKS = TOKENS // BLOCK
+SEQ_BLOCKS = SEQ // BLOCK
+TILES = TOKENS // P
+EPS = 1e-6
+
+FLOPS = 2 * TOKENS * K * HEADS * HEAD
+
+
+def tile_mla_pb_t_kernel(tc, x, wq_words, wq_scales, q_norm_w, freqs_cos, freqs_sin, out):
+    nc = tc.nc
+    x_blocks = x.rearrange("b t k -> (b t) k").rearrange("(c p n) k -> c p n k", p=P, n=TILES_IN_BLOCK)
+    out_blocks = out.rearrange("b t h d -> (b t) (h d)").rearrange("(c p n) f -> c p n f", p=P, n=TILES_IN_BLOCK)
+
+    with ExitStack() as ctx:
+        const = ctx.enter_context(tc.tile_pool(name="const", bufs=1))
+        x_pool = ctx.enter_context(tc.tile_pool(name="x_pool", bufs=BLOCKS))
+        quant = ctx.enter_context(tc.tile_pool(name="quant", bufs=3))
+        stats = ctx.enter_context(tc.tile_pool(name="stats", bufs=4))
+        work = ctx.enter_context(tc.tile_pool(name="work", bufs=3))
+        psum_t = ctx.enter_context(tc.psum_pool(name="psum_t", bufs=2))
+        psum_q = ctx.enter_context(tc.psum_pool(name="psum_q", bufs=6))
+
+        w_scales = const.tile([P, PASSES, HEADS * HEAD], U8, align_bytes=64)
+        nc.vector.memset(w_scales[:].bitcast(I32), 0)
+        scale_rows = wq_scales.bitcast(I32).rearrange("g q w -> q g w")
+        for quadrant in range(4):
+            nc.sync.dma_start(
+                out=w_scales[32 * quadrant : 32 * quadrant + 4].bitcast(I32),
+                in_=scale_rows[4 * quadrant : 4 * quadrant + 4],
+            )
+
+        x_tiles = []
+        x_first = x_pool.tile([P, TILES_IN_BLOCK, K], BF16, name="x_block", tag="x_block")
+        nc.sync.dma_start(out=x_first[:], in_=x_blocks[0])
+        x_tiles.append(x_first)
+
+        w_words = const.tile([P, PASSES, 2 * HEADS * HEAD], U8, align_bytes=64)
+        nc.sync.dma_start(out=w_words[:].bitcast(I32), in_=wq_words.bitcast(I32).rearrange("g p w -> p g w"))
+
+        for block in range(1, BLOCKS):
+            x_block = x_pool.tile([P, TILES_IN_BLOCK, K], BF16, name="x_block", tag="x_block")
+            nc.sync.dma_start(out=x_block[:], in_=x_blocks[block])
+            x_tiles.append(x_block)
+
+        identity = const.tile([P, P], F32)
+        make_identity(nc, identity[:])
+        eps = const.tile([P, 1], F32)
+        nc.vector.memset(eps[:], EPS)
+        warm = const.tile([P, 1], F32)
+        nc.scalar.activation(out=warm[:], in_=eps[:], func=ACT.Sqrt)
+
+        gain = const.tile([P, PAIRS, 2], BF16)
+        nc.scalar.dma_start(out=gain[:].rearrange("p j e -> p (j e)"), in_=q_norm_w.partition_broadcast(P))
+        cos = const.tile([P, SEQ_BLOCKS, TILES_IN_BLOCK * PAIRS], BF16)
+        sin = const.tile([P, SEQ_BLOCKS, TILES_IN_BLOCK * PAIRS], BF16)
+        nc.scalar.dma_start(out=cos[:], in_=freqs_cos.rearrange("(c p n) j -> p c (n j)", p=P, n=TILES_IN_BLOCK))
+        nc.scalar.dma_start(out=sin[:], in_=freqs_sin.rearrange("(c p n) j -> p c (n j)", p=P, n=TILES_IN_BLOCK))
+        seq_tiles = SEQ_BLOCKS * TILES_IN_BLOCK
+        minus_gain_b = const.tile([P, 1, PAIRS], F32)
+        nc.vector.tensor_scalar_mul(out=minus_gain_b[:, 0, :], in0=gain[:, :, 1], scalar1=-1.0)
+        gain_a = gain[:, :, 0].unsqueeze(1).to_broadcast([P, seq_tiles, PAIRS])
+        gain_b = gain[:, :, 1].unsqueeze(1).to_broadcast([P, seq_tiles, PAIRS])
+        cos_rows = cos[:].rearrange("p c (n j) -> p (c n) j", j=PAIRS)
+        sin_rows = sin[:].rearrange("p c (n j) -> p (c n) j", j=PAIRS)
+        from_a = const.tile([P, seq_tiles, 2, PAIRS], F32)
+        from_b = const.tile([P, seq_tiles, 2, PAIRS], F32)
+        nc.vector.tensor_tensor(out=from_a[:, :, 0, :], in0=cos_rows, in1=gain_a, op=ALU.mult)
+        nc.vector.tensor_tensor(out=from_a[:, :, 1, :], in0=sin_rows, in1=gain_a, op=ALU.mult)
+        nc.vector.tensor_tensor(
+            out=from_b[:, :, 0, :], in0=sin_rows, in1=minus_gain_b[:].to_broadcast([P, seq_tiles, PAIRS]), op=ALU.mult
+        )
+        nc.vector.tensor_tensor(out=from_b[:, :, 1, :], in0=cos_rows, in1=gain_b, op=ALU.mult)
+
+        grouped_of = {}
+        q_of = {}
+
+        def transpose_tile(i):
+            x_words = x_tiles[i // TILES_IN_BLOCK][:, i % TILES_IN_BLOCK, :].bitcast(F32)
+            flipped = psum_t.tile([P, PASSES, 2, P], F32)
+            for g in range(PASSES):
+                for u in range(2):
+                    nc.tensor.transpose(flipped[:, g, u, :], x_words[:, WORDS * g + u : WORDS * (g + 1) : 2], identity[:])
+            grouped = quant.tile([P, PASSES * P * 4], BF16, align_bytes=64)
+            nc.scalar.copy(
+                out=grouped[:].bitcast(F32).rearrange("p (g r u) -> p g r u", g=PASSES, u=2),
+                in_=flipped[:].rearrange("p g u r -> p g r u"),
+            )
+            grouped_of[i] = grouped
+
+        def multiply_tile(i):
+            x_codes = quant.tile([P, PASSES, P], U32, align_bytes=64)
+            x_scales = quant.tile([P, PASSES, P], U8, align_bytes=64)
+            nc.vector.quantize_mx(
+                out=x_codes[:].rearrange("p g r -> p (g r)").bitcast(FP8X4),
+                scales=x_scales[:].rearrange("p g r -> p (g r)"),
+                in_=grouped_of[i][:],
+            )
+            banks = []
+            for bank in range(BANKS):
+                q = psum_q.tile([P, BANK], F32)
+                for g in range(PASSES):
+                    nc.tensor.matmul_mx(
+                        out=q[:],
+                        lhsT=x_codes[:, g, :].bitcast(FP8X4),
+                        lhsT_scale=x_scales[:, g, :],
+                        rhs=w_words[:, g, 2 * BANK * bank : 2 * BANK * (bank + 1)].bitcast(FP4X4),
+                        rhs_scale=w_scales[:, g, BANK * bank : BANK * (bank + 1)],
+                        start=(g == 0),
+                        stop=(g == PASSES - 1),
+                    )
+                banks.append(q)
+            q_of[i] = banks
+
+        def finish_tile(i):
+            banks = q_of[i]
+            sum_sq = stats.tile([P, HEADS], F32)
+            for h in range(HEADS):
+                squares = work.tile([P, HEAD], F32)
+                nc.scalar.activation(
+                    out=squares[:],
+                    in_=banks[h // BANK_HEADS][:, HEAD * (h % BANK_HEADS) : HEAD * (h % BANK_HEADS + 1)],
+                    func=ACT.Square,
+                    accum_out=sum_sq[:, h : h + 1],
+                )
+            rms = stats.tile([P, HEADS], F32)
+            nc.scalar.activation(out=rms[:], in_=sum_sq[:], func=ACT.Sqrt, scale=1.0 / HEAD, bias=eps[:, 0:1])
+            r = stats.tile([P, HEADS], F32)
+            nc.vector.reciprocal(out=r[:], in_=rms[:])
+
+            seq_tile = i % seq_tiles
+            part_a = work.tile([P, HEADS, 2, PAIRS], F32)
+            part_b = work.tile([P, HEADS, 2, PAIRS], F32)
+            result = work.tile([P, HEADS, PAIRS, 2], F32)
+            for bank in range(BANKS):
+                pairs = banks[bank][:].rearrange("p (h j e) -> p h e j", h=BANK_HEADS, e=2)
+                first, last = BANK_HEADS * bank, BANK_HEADS * (bank + 1)
+                for h in range(first, last):
+                    for e, part, table in ((0, part_a, from_a), (1, part_b, from_b)):
+                        nc.vector.scalar_tensor_tensor(
+                            out=part[:, h, :, :],
+                            in0=pairs[:, h % BANK_HEADS, e : e + 1, :].to_broadcast([P, 2, PAIRS]),
+                            scalar=r[:, h : h + 1],
+                            in1=table[:, seq_tile, :, :],
+                            op0=ALU.mult,
+                            op1=ALU.mult,
+                        )
+                nc.gpsimd.tensor_tensor(
+                    out=result[:, first:last, :, :],
+                    in0=part_a[:, first:last, :, :].rearrange("p h e j -> p h j e"),
+                    in1=part_b[:, first:last, :, :].rearrange("p h e j -> p h j e"),
+                    op=ALU.add,
+                )
+            nc.sync.dma_start(
+                out=out_blocks[i // TILES_IN_BLOCK][:, i % TILES_IN_BLOCK, :],
+                in_=result[:].rearrange("p h j e -> p (h j e)"),
+            )
+
+        for step in range(TILES + 2):
+            if step < TILES:
+                transpose_tile(step)
+            if 1 <= step <= TILES:
+                multiply_tile(step - 1)
+            if step >= 2:
+                finish_tile(step - 2)

@@ -79,27 +79,32 @@ def tile_mla_pb_t_kernel(tc, x, wq_words, wq_scales, q_norm_w, freqs_cos, freqs_
         warm = const.tile([P, 1], F32)
         nc.scalar.activation(out=warm[:], in_=eps[:], func=ACT.Sqrt)
 
+        seq_tiles = SEQ_BLOCKS * TILES_IN_BLOCK
         gain = const.tile([P, PAIRS, 2], BF16)
         nc.scalar.dma_start(out=gain[:].rearrange("p j e -> p (j e)"), in_=q_norm_w.partition_broadcast(P))
-        cos = const.tile([P, SEQ_BLOCKS, TILES_IN_BLOCK * PAIRS], BF16)
-        sin = const.tile([P, SEQ_BLOCKS, TILES_IN_BLOCK * PAIRS], BF16)
-        nc.scalar.dma_start(out=cos[:], in_=freqs_cos.rearrange("(c p n) j -> p c (n j)", p=P, n=TILES_IN_BLOCK))
-        nc.scalar.dma_start(out=sin[:], in_=freqs_sin.rearrange("(c p n) j -> p c (n j)", p=P, n=TILES_IN_BLOCK))
-        seq_tiles = SEQ_BLOCKS * TILES_IN_BLOCK
-        minus_gain_b = const.tile([P, 1, PAIRS], F32)
-        nc.vector.tensor_scalar_mul(out=minus_gain_b[:, 0, :], in0=gain[:, :, 1], scalar1=-1.0)
-        gain_a = gain[:, :, 0].unsqueeze(1).to_broadcast([P, seq_tiles, PAIRS])
-        gain_b = gain[:, :, 1].unsqueeze(1).to_broadcast([P, seq_tiles, PAIRS])
-        cos_rows = cos[:].rearrange("p c (n j) -> p (c n) j", j=PAIRS)
-        sin_rows = sin[:].rearrange("p c (n j) -> p (c n) j", j=PAIRS)
-        from_a = const.tile([P, seq_tiles, 2, PAIRS], F32)
-        from_b = const.tile([P, seq_tiles, 2, PAIRS], F32)
-        nc.vector.tensor_tensor(out=from_a[:, :, 0, :], in0=cos_rows, in1=gain_a, op=ALU.mult)
-        nc.vector.tensor_tensor(out=from_a[:, :, 1, :], in0=sin_rows, in1=gain_a, op=ALU.mult)
+        trig = const.tile([P, 3, seq_tiles, PAIRS], BF16)
+        for plane, freqs in enumerate((freqs_cos, freqs_sin, freqs_cos)):
+            nc.scalar.dma_start(
+                out=trig[:, plane, :, :].rearrange("p (c n) j -> p c (n j)", n=TILES_IN_BLOCK),
+                in_=freqs.rearrange("(c p n) j -> p c (n j)", p=P, n=TILES_IN_BLOCK),
+            )
+        signed_gain_b = const.tile([P, PAIRS, 2], F32)
+        nc.vector.tensor_scalar_mul(out=signed_gain_b[:, :, 0], in0=gain[:, :, 1], scalar1=-1.0)
+        nc.vector.tensor_copy(out=signed_gain_b[:, :, 1], in_=gain[:, :, 1])
+        from_a = const.tile([P, seq_tiles, PAIRS, 2], F32)
+        from_b = const.tile([P, seq_tiles, PAIRS, 2], F32)
         nc.vector.tensor_tensor(
-            out=from_b[:, :, 0, :], in0=sin_rows, in1=minus_gain_b[:].to_broadcast([P, seq_tiles, PAIRS]), op=ALU.mult
+            out=from_a[:],
+            in0=trig[:, 0:2, :, :].rearrange("p e s j -> p s j e"),
+            in1=gain[:, :, 0:1].unsqueeze(1).to_broadcast([P, seq_tiles, PAIRS, 2]),
+            op=ALU.mult,
         )
-        nc.vector.tensor_tensor(out=from_b[:, :, 1, :], in0=cos_rows, in1=gain_b, op=ALU.mult)
+        nc.vector.tensor_tensor(
+            out=from_b[:],
+            in0=trig[:, 1:3, :, :].rearrange("p e s j -> p s j e"),
+            in1=signed_gain_b[:].unsqueeze(1).to_broadcast([P, seq_tiles, PAIRS, 2]),
+            op=ALU.mult,
+        )
 
         grouped_of = {}
         q_of = {}
@@ -158,17 +163,17 @@ def tile_mla_pb_t_kernel(tc, x, wq_words, wq_scales, q_norm_w, freqs_cos, freqs_
             nc.vector.reciprocal(out=r[:], in_=rms[:])
 
             seq_tile = i % seq_tiles
-            part_a = work.tile([P, HEADS, 2, PAIRS], F32)
-            part_b = work.tile([P, HEADS, 2, PAIRS], F32)
+            part_a = work.tile([P, HEADS, PAIRS, 2], F32)
+            part_b = work.tile([P, HEADS, PAIRS, 2], F32)
             result = work.tile([P, HEADS, PAIRS, 2], F32)
             for bank in range(BANKS):
-                pairs = banks[bank][:].rearrange("p (h j e) -> p h e j", h=BANK_HEADS, e=2)
+                pairs = banks[bank][:].rearrange("p (h j e) -> p h j e", h=BANK_HEADS, e=2)
                 first, last = BANK_HEADS * bank, BANK_HEADS * (bank + 1)
                 for h in range(first, last):
                     for e, part, table in ((0, part_a, from_a), (1, part_b, from_b)):
                         nc.vector.scalar_tensor_tensor(
                             out=part[:, h, :, :],
-                            in0=pairs[:, h % BANK_HEADS, e : e + 1, :].to_broadcast([P, 2, PAIRS]),
+                            in0=pairs[:, h - first, :, e : e + 1].to_broadcast([P, PAIRS, 2]),
                             scalar=r[:, h : h + 1],
                             in1=table[:, seq_tile, :, :],
                             op0=ALU.mult,
@@ -176,8 +181,8 @@ def tile_mla_pb_t_kernel(tc, x, wq_words, wq_scales, q_norm_w, freqs_cos, freqs_
                         )
                 nc.gpsimd.tensor_tensor(
                     out=result[:, first:last, :, :],
-                    in0=part_a[:, first:last, :, :].rearrange("p h e j -> p h j e"),
-                    in1=part_b[:, first:last, :, :].rearrange("p h e j -> p h j e"),
+                    in0=part_a[:, first:last, :, :],
+                    in1=part_b[:, first:last, :, :],
                     op=ALU.add,
                 )
             nc.sync.dma_start(

@@ -32,6 +32,7 @@ BLOCKS = TOKENS // BLOCK
 SEQ_BLOCKS = SEQ // BLOCK
 TILES = TOKENS // P
 EPS = 1e-6
+Q_TILES_IN_FLIGHT = 3
 
 FLOPS = 2 * TOKENS * K * HEADS * HEAD
 
@@ -42,13 +43,20 @@ def tile_mla_pb_t_kernel(tc, x, wq_words, wq_scales, q_norm_w, freqs_cos, freqs_
     out_blocks = out.rearrange("b t h d -> (b t) (h d)").rearrange("(c p n) f -> c p n f", p=P, n=TILES_IN_BLOCK)
 
     with ExitStack() as ctx:
+        ctx.enter_context(tc.manual_schedule())
         const = ctx.enter_context(tc.tile_pool(name="const", bufs=1))
         x_pool = ctx.enter_context(tc.tile_pool(name="x_pool", bufs=BLOCKS))
         quant = ctx.enter_context(tc.tile_pool(name="quant", bufs=3))
         stats = ctx.enter_context(tc.tile_pool(name="stats", bufs=4))
         work = ctx.enter_context(tc.tile_pool(name="work", bufs=3))
         psum_t = ctx.enter_context(tc.psum_pool(name="psum_t", bufs=2))
-        psum_q = ctx.enter_context(tc.psum_pool(name="psum_q", bufs=6))
+        psum_q = ctx.enter_context(tc.psum_pool(name="psum_q", bufs=Q_TILES_IN_FLIGHT * BANKS))
+
+        x_tiles = []
+        for block in range(BLOCKS):
+            x_block = x_pool.tile([P, TILES_IN_BLOCK, K], BF16, name="x_block", tag="x_block")
+            x_tiles.append(x_block)
+        nc.sync.dma_start(out=x_tiles[0][:, 0, :], in_=x_blocks[0][:, 0, :])
 
         w_scales = const.tile([P, PASSES, HEADS * HEAD], U8, align_bytes=64)
         nc.vector.memset(w_scales[:].bitcast(I32), 0)
@@ -58,26 +66,20 @@ def tile_mla_pb_t_kernel(tc, x, wq_words, wq_scales, q_norm_w, freqs_cos, freqs_
                 out=w_scales[32 * quadrant : 32 * quadrant + 4].bitcast(I32),
                 in_=scale_rows[4 * quadrant : 4 * quadrant + 4],
             )
-
-        x_tiles = []
-        x_first = x_pool.tile([P, TILES_IN_BLOCK, K], BF16, name="x_block", tag="x_block")
-        nc.sync.dma_start(out=x_first[:], in_=x_blocks[0])
-        x_tiles.append(x_first)
-
         w_words = const.tile([P, PASSES, 2 * HEADS * HEAD], U8, align_bytes=64)
         nc.sync.dma_start(out=w_words[:].bitcast(I32), in_=wq_words.bitcast(I32).rearrange("g p w -> p g w"))
 
+        for n in range(1, TILES_IN_BLOCK):
+            nc.sync.dma_start(out=x_tiles[0][:, n, :], in_=x_blocks[0][:, n, :])
         for block in range(1, BLOCKS):
-            x_block = x_pool.tile([P, TILES_IN_BLOCK, K], BF16, name="x_block", tag="x_block")
-            nc.sync.dma_start(out=x_block[:], in_=x_blocks[block])
-            x_tiles.append(x_block)
+            nc.sync.dma_start(out=x_tiles[block][:], in_=x_blocks[block])
 
         identity = const.tile([P, P], F32)
         make_identity(nc, identity[:])
         eps = const.tile([P, 1], F32)
         nc.vector.memset(eps[:], EPS)
         warm = const.tile([P, 1], F32)
-        nc.scalar.activation(out=warm[:], in_=eps[:], func=ACT.Sqrt)
+        nc.scalar.activation(out=warm[:], in_=eps[:], func=ACT.Abs_reciprocal_sqrt)
 
         seq_tiles = SEQ_BLOCKS * TILES_IN_BLOCK
         gain = const.tile([P, PAIRS, 2], BF16)
@@ -88,26 +90,29 @@ def tile_mla_pb_t_kernel(tc, x, wq_words, wq_scales, q_norm_w, freqs_cos, freqs_
                 out=trig[:, plane, :, :].rearrange("p (c n) j -> p c (n j)", n=TILES_IN_BLOCK),
                 in_=freqs.rearrange("(c p n) j -> p c (n j)", p=P, n=TILES_IN_BLOCK),
             )
-        signed_gain_b = const.tile([P, PAIRS, 2], F32)
-        nc.vector.tensor_scalar_mul(out=signed_gain_b[:, :, 0], in0=gain[:, :, 1], scalar1=-1.0)
-        nc.vector.tensor_copy(out=signed_gain_b[:, :, 1], in_=gain[:, :, 1])
         from_a = const.tile([P, seq_tiles, PAIRS, 2], F32)
         from_b = const.tile([P, seq_tiles, PAIRS, 2], F32)
-        nc.vector.tensor_tensor(
-            out=from_a[:],
-            in0=trig[:, 0:2, :, :].rearrange("p e s j -> p s j e"),
-            in1=gain[:, :, 0:1].unsqueeze(1).to_broadcast([P, seq_tiles, PAIRS, 2]),
-            op=ALU.mult,
-        )
-        nc.vector.tensor_tensor(
-            out=from_b[:],
-            in0=trig[:, 1:3, :, :].rearrange("p e s j -> p s j e"),
-            in1=signed_gain_b[:].unsqueeze(1).to_broadcast([P, seq_tiles, PAIRS, 2]),
-            op=ALU.mult,
-        )
+
+        def build_tables():
+            signed_gain_b = const.tile([P, PAIRS, 2], F32)
+            nc.vector.tensor_scalar_mul(out=signed_gain_b[:, :, 0], in0=gain[:, :, 1], scalar1=-1.0)
+            nc.vector.tensor_copy(out=signed_gain_b[:, :, 1], in_=gain[:, :, 1])
+            nc.vector.tensor_tensor(
+                out=from_a[:],
+                in0=trig[:, 0:2, :, :].rearrange("p e s j -> p s j e"),
+                in1=gain[:, :, 0:1].unsqueeze(1).to_broadcast([P, seq_tiles, PAIRS, 2]),
+                op=ALU.mult,
+            )
+            nc.vector.tensor_tensor(
+                out=from_b[:],
+                in0=trig[:, 1:3, :, :].rearrange("p e s j -> p s j e"),
+                in1=signed_gain_b[:].unsqueeze(1).to_broadcast([P, seq_tiles, PAIRS, 2]),
+                op=ALU.mult,
+            )
 
         grouped_of = {}
         q_of = {}
+        r_of = {}
 
         def transpose_tile(i):
             x_words = x_tiles[i // TILES_IN_BLOCK][:, i % TILES_IN_BLOCK, :].bitcast(F32)
@@ -146,54 +151,51 @@ def tile_mla_pb_t_kernel(tc, x, wq_words, wq_scales, q_norm_w, freqs_cos, freqs_
                 banks.append(q)
             q_of[i] = banks
 
-        def finish_tile(i):
-            banks = q_of[i]
+        def norm_tile(i):
             sum_sq = stats.tile([P, HEADS], F32)
             for h in range(HEADS):
                 squares = work.tile([P, HEAD], F32)
                 nc.scalar.activation(
                     out=squares[:],
-                    in_=banks[h // BANK_HEADS][:, HEAD * (h % BANK_HEADS) : HEAD * (h % BANK_HEADS + 1)],
+                    in_=q_of[i][h // BANK_HEADS][:, HEAD * (h % BANK_HEADS) : HEAD * (h % BANK_HEADS + 1)],
                     func=ACT.Square,
                     accum_out=sum_sq[:, h : h + 1],
                 )
-            rms = stats.tile([P, HEADS], F32)
-            nc.scalar.activation(out=rms[:], in_=sum_sq[:], func=ACT.Sqrt, scale=1.0 / HEAD, bias=eps[:, 0:1])
             r = stats.tile([P, HEADS], F32)
-            nc.vector.reciprocal(out=r[:], in_=rms[:])
+            nc.scalar.activation(
+                out=r[:], in_=sum_sq[:], func=ACT.Abs_reciprocal_sqrt, scale=1.0 / HEAD, bias=eps[:, 0:1]
+            )
+            r_of[i] = r
 
-            seq_tile = i % seq_tiles
+        def rotate_tile(i):
             part_a = work.tile([P, HEADS, PAIRS, 2], F32)
             part_b = work.tile([P, HEADS, PAIRS, 2], F32)
+            for h in range(HEADS):
+                pairs = q_of[i][h // BANK_HEADS][:].rearrange("p (h j e) -> p h j e", h=BANK_HEADS, e=2)
+                for e, part, table in ((0, part_a, from_a), (1, part_b, from_b)):
+                    nc.vector.scalar_tensor_tensor(
+                        out=part[:, h, :, :],
+                        in0=pairs[:, h % BANK_HEADS, :, e : e + 1].to_broadcast([P, PAIRS, 2]),
+                        scalar=r_of[i][:, h : h + 1],
+                        in1=table[:, i % seq_tiles, :, :],
+                        op0=ALU.mult,
+                        op1=ALU.mult,
+                    )
             result = work.tile([P, HEADS, PAIRS, 2], F32)
-            for bank in range(BANKS):
-                pairs = banks[bank][:].rearrange("p (h j e) -> p h j e", h=BANK_HEADS, e=2)
-                first, last = BANK_HEADS * bank, BANK_HEADS * (bank + 1)
-                for h in range(first, last):
-                    for e, part, table in ((0, part_a, from_a), (1, part_b, from_b)):
-                        nc.vector.scalar_tensor_tensor(
-                            out=part[:, h, :, :],
-                            in0=pairs[:, h - first, :, e : e + 1].to_broadcast([P, PAIRS, 2]),
-                            scalar=r[:, h : h + 1],
-                            in1=table[:, seq_tile, :, :],
-                            op0=ALU.mult,
-                            op1=ALU.mult,
-                        )
-                nc.gpsimd.tensor_tensor(
-                    out=result[:, first:last, :, :],
-                    in0=part_a[:, first:last, :, :],
-                    in1=part_b[:, first:last, :, :],
-                    op=ALU.add,
-                )
+            nc.gpsimd.tensor_tensor(out=result[:], in0=part_a[:], in1=part_b[:], op=ALU.add)
             nc.sync.dma_start(
                 out=out_blocks[i // TILES_IN_BLOCK][:, i % TILES_IN_BLOCK, :],
                 in_=result[:].rearrange("p h j e -> p (h j e)"),
             )
 
-        for step in range(TILES + 2):
+        for step in range(TILES + 3):
             if step < TILES:
                 transpose_tile(step)
             if 1 <= step <= TILES:
                 multiply_tile(step - 1)
-            if step >= 2:
-                finish_tile(step - 2)
+            if step == 1:
+                build_tables()
+            if 2 <= step <= TILES + 1:
+                norm_tile(step - 2)
+            if step >= 3:
+                rotate_tile(step - 3)

@@ -84,29 +84,22 @@ def tile_mla_pb_t_kernel(tc, x, wq_words, wq_scales, q_norm_w, freqs_cos, freqs_
         seq_tiles = SEQ_BLOCKS * TILES_IN_BLOCK
         gain = const.tile([P, PAIRS, 2], BF16)
         nc.scalar.dma_start(out=gain[:].rearrange("p j e -> p (j e)"), in_=q_norm_w.partition_broadcast(P))
-        trig = const.tile([P, 3, seq_tiles, PAIRS], BF16)
-        for plane, freqs in enumerate((freqs_cos, freqs_sin, freqs_cos)):
+        trig = const.tile([P, 2, 2, seq_tiles, PAIRS], BF16)
+        for plane, freqs in enumerate((freqs_cos, freqs_sin, freqs_sin, freqs_cos)):
             nc.scalar.dma_start(
-                out=trig[:, plane, :, :].rearrange("p (c n) j -> p c (n j)", n=TILES_IN_BLOCK),
+                out=trig[:, plane // 2, plane % 2, :, :].rearrange("p (c n) j -> p c (n j)", n=TILES_IN_BLOCK),
                 in_=freqs.rearrange("(c p n) j -> p c (n j)", p=P, n=TILES_IN_BLOCK),
             )
-        from_a = const.tile([P, seq_tiles, PAIRS, 2], F32)
-        from_b = const.tile([P, seq_tiles, PAIRS, 2], F32)
+        table = const.tile([P, seq_tiles, PAIRS, 2, 2], F32)
 
-        def build_tables():
-            signed_gain_b = const.tile([P, PAIRS, 2], F32)
-            nc.vector.tensor_scalar_mul(out=signed_gain_b[:, :, 0], in0=gain[:, :, 1], scalar1=-1.0)
-            nc.vector.tensor_copy(out=signed_gain_b[:, :, 1], in_=gain[:, :, 1])
+        def build_table():
+            signed_gain = const.tile([P, PAIRS, 2, 2], F32)
+            nc.vector.tensor_copy(out=signed_gain[:], in_=gain[:].unsqueeze(3).to_broadcast([P, PAIRS, 2, 2]))
+            nc.vector.tensor_scalar_mul(out=signed_gain[:, :, 1, 0], in0=signed_gain[:, :, 1, 0], scalar1=-1.0)
             nc.vector.tensor_tensor(
-                out=from_a[:],
-                in0=trig[:, 0:2, :, :].rearrange("p e s j -> p s j e"),
-                in1=gain[:, :, 0:1].unsqueeze(1).to_broadcast([P, seq_tiles, PAIRS, 2]),
-                op=ALU.mult,
-            )
-            nc.vector.tensor_tensor(
-                out=from_b[:],
-                in0=trig[:, 1:3, :, :].rearrange("p e s j -> p s j e"),
-                in1=signed_gain_b[:].unsqueeze(1).to_broadcast([P, seq_tiles, PAIRS, 2]),
+                out=table[:],
+                in0=trig[:].rearrange("p i e s j -> p s j i e"),
+                in1=signed_gain[:].unsqueeze(1).to_broadcast([P, seq_tiles, PAIRS, 2, 2]),
                 op=ALU.mult,
             )
 
@@ -153,36 +146,40 @@ def tile_mla_pb_t_kernel(tc, x, wq_words, wq_scales, q_norm_w, freqs_cos, freqs_
 
         def norm_tile(i):
             sum_sq = stats.tile([P, HEADS], F32)
-            for h in range(HEADS):
-                squares = work.tile([P, HEAD], F32)
-                nc.scalar.activation(
-                    out=squares[:],
-                    in_=q_of[i][h // BANK_HEADS][:, HEAD * (h % BANK_HEADS) : HEAD * (h % BANK_HEADS + 1)],
-                    func=ACT.Square,
-                    accum_out=sum_sq[:, h : h + 1],
-                )
             r = stats.tile([P, HEADS], F32)
-            nc.scalar.activation(
-                out=r[:], in_=sum_sq[:], func=ACT.Abs_reciprocal_sqrt, scale=1.0 / HEAD, bias=eps[:, 0:1]
-            )
+            for bank in range(BANKS):
+                first, last = BANK_HEADS * bank, BANK_HEADS * (bank + 1)
+                for h in range(first, last):
+                    squares = work.tile([P, HEAD], F32)
+                    nc.scalar.activation(
+                        out=squares[:],
+                        in_=q_of[i][bank][:, HEAD * (h - first) : HEAD * (h - first + 1)],
+                        func=ACT.Square,
+                        accum_out=sum_sq[:, h : h + 1],
+                    )
+                nc.scalar.activation(
+                    out=r[:, first:last],
+                    in_=sum_sq[:, first:last],
+                    func=ACT.Abs_reciprocal_sqrt,
+                    scale=1.0 / HEAD,
+                    bias=eps[:, 0:1],
+                )
             r_of[i] = r
 
         def rotate_tile(i):
-            part_a = work.tile([P, HEADS, PAIRS, 2], F32)
-            part_b = work.tile([P, HEADS, PAIRS, 2], F32)
+            parts = work.tile([P, HEADS, PAIRS, 2, 2], F32)
             for h in range(HEADS):
-                pairs = q_of[i][h // BANK_HEADS][:].rearrange("p (h j e) -> p h j e", h=BANK_HEADS, e=2)
-                for e, part, table in ((0, part_a, from_a), (1, part_b, from_b)):
-                    nc.vector.scalar_tensor_tensor(
-                        out=part[:, h, :, :],
-                        in0=pairs[:, h % BANK_HEADS, :, e : e + 1].to_broadcast([P, PAIRS, 2]),
-                        scalar=r_of[i][:, h : h + 1],
-                        in1=table[:, i % seq_tiles, :, :],
-                        op0=ALU.mult,
-                        op1=ALU.mult,
-                    )
+                q_head = q_of[i][h // BANK_HEADS][:, HEAD * (h % BANK_HEADS) : HEAD * (h % BANK_HEADS + 1)]
+                nc.vector.scalar_tensor_tensor(
+                    out=parts[:, h, :, :, :].rearrange("p j i e -> p (j i) e"),
+                    in0=q_head.unsqueeze(2).to_broadcast([P, HEAD, 2]),
+                    scalar=r_of[i][:, h : h + 1],
+                    in1=table[:, i % seq_tiles, :, :, :].rearrange("p j i e -> p (j i) e"),
+                    op0=ALU.mult,
+                    op1=ALU.mult,
+                )
             result = work.tile([P, HEADS, PAIRS, 2], F32)
-            nc.gpsimd.tensor_tensor(out=result[:], in0=part_a[:], in1=part_b[:], op=ALU.add)
+            nc.gpsimd.tensor_tensor(out=result[:], in0=parts[:, :, :, 0, :], in1=parts[:, :, :, 1, :], op=ALU.add)
             nc.sync.dma_start(
                 out=out_blocks[i // TILES_IN_BLOCK][:, i % TILES_IN_BLOCK, :],
                 in_=result[:].rearrange("p h j e -> p (h j e)"),
@@ -194,7 +191,7 @@ def tile_mla_pb_t_kernel(tc, x, wq_words, wq_scales, q_norm_w, freqs_cos, freqs_
             if 1 <= step <= TILES:
                 multiply_tile(step - 1)
             if step == 1:
-                build_tables()
+                build_table()
             if 2 <= step <= TILES + 1:
                 norm_tile(step - 2)
             if step >= 3:

@@ -34,6 +34,8 @@ TILES = TOKENS // P
 EPS = 1e-6
 Q_TILES_IN_FLIGHT = 3
 
+LOAD_AHEAD = 6
+
 FLOPS = 2 * TOKENS * K * HEADS * HEAD
 
 
@@ -71,35 +73,38 @@ def tile_mla_pb_t_kernel(tc, x, wq_words, wq_scales, q_norm_w, freqs_cos, freqs_
 
         for n in range(1, TILES_IN_BLOCK):
             nc.sync.dma_start(out=x_tiles[0][:, n, :], in_=x_blocks[0][:, n, :])
-        for block in range(1, BLOCKS):
-            nc.sync.dma_start(out=x_tiles[block][:], in_=x_blocks[block])
+        nc.sync.dma_start(out=x_tiles[1][:], in_=x_blocks[1])
 
         identity = const.tile([P, P], F32)
         make_identity(nc, identity[:])
         eps = const.tile([P, 1], F32)
         nc.vector.memset(eps[:], EPS)
-        warm = const.tile([P, 1], F32)
-        nc.scalar.activation(out=warm[:], in_=eps[:], func=ACT.Abs_reciprocal_sqrt)
-
         seq_tiles = SEQ_BLOCKS * TILES_IN_BLOCK
         gain = const.tile([P, PAIRS, 2], BF16)
         nc.scalar.dma_start(out=gain[:].rearrange("p j e -> p (j e)"), in_=q_norm_w.partition_broadcast(P))
         trig = const.tile([P, 2, 2, seq_tiles, PAIRS], BF16)
-        for plane, freqs in enumerate((freqs_cos, freqs_sin, freqs_sin, freqs_cos)):
+        for plane, freqs in enumerate((freqs_cos, freqs_sin)):
             nc.scalar.dma_start(
-                out=trig[:, plane // 2, plane % 2, :, :].rearrange("p (c n) j -> p c (n j)", n=TILES_IN_BLOCK),
+                out=trig[:, 0, plane, :, :].rearrange("p (c n) j -> p c (n j)", n=TILES_IN_BLOCK),
                 in_=freqs.rearrange("(c p n) j -> p c (n j)", p=P, n=TILES_IN_BLOCK),
             )
-        table = const.tile([P, seq_tiles, PAIRS, 2, 2], F32)
+        warm = const.tile([P, 1], F32)
+        nc.scalar.activation(out=warm[:], in_=eps[:], func=ACT.Abs_reciprocal_sqrt)
 
-        def build_table():
-            signed_gain = const.tile([P, PAIRS, 2, 2], F32)
+        table = const.tile([P, seq_tiles, PAIRS, 2, 2], F32)
+        signed_gain = const.tile([P, PAIRS, 2, 2], F32)
+
+        def build_signed_gain():
             nc.vector.tensor_copy(out=signed_gain[:], in_=gain[:].unsqueeze(3).to_broadcast([P, PAIRS, 2, 2]))
             nc.vector.tensor_scalar_mul(out=signed_gain[:, :, 1, 0], in0=signed_gain[:, :, 1, 0], scalar1=-1.0)
+            for e in range(2):
+                nc.vector.tensor_copy(out=trig[:, 1, e, :, :], in_=trig[:, 0, 1 - e, :, :])
+
+        def build_table(s):
             nc.vector.tensor_tensor(
-                out=table[:],
-                in0=trig[:].rearrange("p i e s j -> p s j i e"),
-                in1=signed_gain[:].unsqueeze(1).to_broadcast([P, seq_tiles, PAIRS, 2, 2]),
+                out=table[:, s, :, :, :],
+                in0=trig[:, :, :, s, :].rearrange("p i e j -> p j i e"),
+                in1=signed_gain[:],
                 op=ALU.mult,
             )
 
@@ -107,12 +112,18 @@ def tile_mla_pb_t_kernel(tc, x, wq_words, wq_scales, q_norm_w, freqs_cos, freqs_
         q_of = {}
         r_of = {}
 
+        flipped_of = {}
+
         def transpose_tile(i):
             x_words = x_tiles[i // TILES_IN_BLOCK][:, i % TILES_IN_BLOCK, :].bitcast(F32)
             flipped = psum_t.tile([P, PASSES, 2, P], F32)
             for g in range(PASSES):
                 for u in range(2):
                     nc.tensor.transpose(flipped[:, g, u, :], x_words[:, WORDS * g + u : WORDS * (g + 1) : 2], identity[:])
+            flipped_of[i] = flipped
+
+        def group_tile(i):
+            flipped = flipped_of[i]
             grouped = quant.tile([P, PASSES * P * 4], BF16, align_bytes=64)
             nc.scalar.copy(
                 out=grouped[:].bitcast(F32).rearrange("p (g r u) -> p g r u", g=PASSES, u=2),
@@ -185,14 +196,24 @@ def tile_mla_pb_t_kernel(tc, x, wq_words, wq_scales, q_norm_w, freqs_cos, freqs_
                 in_=result[:].rearrange("p h j e -> p (h j e)"),
             )
 
+        table_parts_in_step = {1: range(0, 4), 2: range(4, seq_tiles)}
         for step in range(TILES + 3):
+            if (step + LOAD_AHEAD) % TILES_IN_BLOCK == 0 and 2 <= (step + LOAD_AHEAD) // TILES_IN_BLOCK < BLOCKS:
+                block = (step + LOAD_AHEAD) // TILES_IN_BLOCK
+                nc.sync.dma_start(out=x_tiles[block][:], in_=x_blocks[block])
             if step < TILES:
                 transpose_tile(step)
             if 1 <= step <= TILES:
                 multiply_tile(step - 1)
-            if step == 1:
-                build_table()
             if 2 <= step <= TILES + 1:
                 norm_tile(step - 2)
-            if step >= 3:
+            if step < TILES:
+                group_tile(step)
+            if step == 1:
+                build_signed_gain()
+            for s in table_parts_in_step.get(step, ()):
+                build_table(s)
+            if step == 2:
+                rotate_tile(0)
+            if step >= 4:
                 rotate_tile(step - 3)

@@ -190,11 +190,22 @@ def tile_mla_pb_t_kernel(tc, x, wq_words, wq_scales, q_norm_w, freqs_cos, freqs_
                     op1=ALU.mult,
                 )
             result = work.tile([P, HEADS, PAIRS, 2], F32)
-            nc.gpsimd.tensor_tensor(out=result[:], in0=parts[:, :, :, 0, :], in1=parts[:, :, :, 1, :], op=ALU.add)
-            nc.sync.dma_start(
-                out=out_blocks[i // TILES_IN_BLOCK][:, i % TILES_IN_BLOCK, :],
-                in_=result[:].rearrange("p h j e -> p (h j e)"),
-            )
+            if i < TILES - 1:
+                nc.gpsimd.tensor_tensor(out=result[:], in0=parts[:, :, :, 0, :], in1=parts[:, :, :, 1, :], op=ALU.add)
+                nc.sync.dma_start(
+                    out=out_blocks[i // TILES_IN_BLOCK][:, i % TILES_IN_BLOCK, :],
+                    in_=result[:].rearrange("p h j e -> p (h j e)"),
+                )
+            else:
+                for bank in range(BANKS):
+                    heads = slice(BANK_HEADS * bank, BANK_HEADS * (bank + 1))
+                    nc.vector.tensor_tensor(
+                        out=result[:, heads, :, :], in0=parts[:, heads, :, 0, :], in1=parts[:, heads, :, 1, :], op=ALU.add
+                    )
+                    nc.sync.dma_start(
+                        out=out_blocks[i // TILES_IN_BLOCK][:, i % TILES_IN_BLOCK, BANK * bank : BANK * (bank + 1)],
+                        in_=result[:, heads, :, :].rearrange("p h j e -> p (h j e)"),
+                    )
 
         table_parts_in_step = {1: range(0, 4), 2: range(4, seq_tiles)}
         for step in range(TILES + 3):

@@ -54,6 +54,10 @@ def tile_mla_pb_t_kernel(tc, x, wq_words, wq_scales, q_norm_w, freqs_cos, freqs_
         psum_t = ctx.enter_context(tc.psum_pool(name="psum_t", bufs=2))
         psum_q = ctx.enter_context(tc.psum_pool(name="psum_q", bufs=Q_TILES_IN_FLIGHT * BANKS))
 
+        gain_row = const.tile([P, HEAD], BF16)
+        nc.vector.memset(gain_row[:], 0.0)
+        ones = const.tile([P, P], BF16)
+        nc.vector.memset(ones[:], 1.0)
         x_tiles = []
         for block in range(BLOCKS):
             x_block = x_pool.tile([P, TILES_IN_BLOCK, K], BF16, name="x_block", tag="x_block")
@@ -80,21 +84,28 @@ def tile_mla_pb_t_kernel(tc, x, wq_words, wq_scales, q_norm_w, freqs_cos, freqs_
         eps = const.tile([P, 1], F32)
         nc.vector.memset(eps[:], EPS)
         seq_tiles = SEQ_BLOCKS * TILES_IN_BLOCK
-        gain = const.tile([P, PAIRS, 2], BF16)
-        nc.scalar.dma_start(out=gain[:].rearrange("p j e -> p (j e)"), in_=q_norm_w.partition_broadcast(P))
         trig = const.tile([P, 2, 2, seq_tiles, PAIRS], BF16)
         for plane, freqs in enumerate((freqs_cos, freqs_sin)):
             nc.scalar.dma_start(
                 out=trig[:, 0, plane, :, :].rearrange("p (c n) j -> p c (n j)", n=TILES_IN_BLOCK),
                 in_=freqs.rearrange("(c p n) j -> p c (n j)", p=P, n=TILES_IN_BLOCK),
             )
+        nc.scalar.dma_start(out=gain_row[0:1, :], in_=q_norm_w.unsqueeze(0))
         warm = const.tile([P, 1], F32)
         nc.scalar.activation(out=warm[:], in_=eps[:], func=ACT.Abs_reciprocal_sqrt)
 
         table = const.tile([P, seq_tiles, PAIRS, 2, 2], F32)
         signed_gain = const.tile([P, PAIRS, 2, 2], F32)
 
+        spread = {}
+
+        def spread_gain():
+            gain = psum_t.tile([P, PAIRS, 2], F32, name="flipped", tag="flipped")
+            nc.tensor.matmul(out=gain[:].rearrange("p j i -> p (j i)"), lhsT=ones[:], rhs=gain_row[:], start=True, stop=True)
+            spread["gain"] = gain
+
         def build_signed_gain():
+            gain = spread["gain"]
             nc.vector.tensor_copy(out=signed_gain[:], in_=gain[:].unsqueeze(3).to_broadcast([P, PAIRS, 2, 2]))
             nc.vector.tensor_scalar_mul(out=signed_gain[:, :, 1, 0], in0=signed_gain[:, :, 1, 0], scalar1=-1.0)
             for e in range(2):
@@ -214,6 +225,8 @@ def tile_mla_pb_t_kernel(tc, x, wq_words, wq_scales, q_norm_w, freqs_cos, freqs_
                 nc.sync.dma_start(out=x_tiles[block][:], in_=x_blocks[block])
             if step < TILES:
                 transpose_tile(step)
+            if step == 0:
+                spread_gain()
             if 1 <= step <= TILES:
                 multiply_tile(step - 1)
             if 2 <= step <= TILES + 1:

from contextlib import ExitStack

import concourse.mybir as mybir
from concourse.masks import make_identity

F32 = mybir.dt.float32
BF16 = mybir.dt.bfloat16
I32 = mybir.dt.int32
U32 = mybir.dt.uint32
U8 = mybir.dt.uint8
FP8X4 = mybir.dt.float8_e4m3fn_x4
FP4X4 = mybir.dt.float4_e2m1fn_x4
ACT = mybir.ActivationFunctionType
ALU = mybir.AluOpType

P = 128
TOKENS = 4 * 1024
SEQ = 1024
K = 1024
K_PASS = 512
PASSES = K // K_PASS
WORDS = K_PASS // 2
HEADS = 8
HEAD = 128
PAIRS = HEAD // 2
BANK = 512
BANKS = HEADS * HEAD // BANK
BANK_HEADS = BANK // HEAD
TILES_IN_BLOCK = 4
BLOCK = TILES_IN_BLOCK * P
BLOCKS = TOKENS // BLOCK
SEQ_BLOCKS = SEQ // BLOCK
TILES = TOKENS // P
EPS = 1e-6
Q_TILES_IN_FLIGHT = 3

LOAD_AHEAD = 6

FLOPS = 2 * TOKENS * K * HEADS * HEAD


def tile_mla_pb_t_kernel(tc, x, wq_words, wq_scales, q_norm_w, freqs_cos, freqs_sin, out):
    nc = tc.nc
    x_blocks = x.rearrange("b t k -> (b t) k").rearrange("(c p n) k -> c p n k", p=P, n=TILES_IN_BLOCK)
    out_blocks = out.rearrange("b t h d -> (b t) (h d)").rearrange("(c p n) f -> c p n f", p=P, n=TILES_IN_BLOCK)

    with ExitStack() as ctx:
        ctx.enter_context(tc.manual_schedule())
        const = ctx.enter_context(tc.tile_pool(name="const", bufs=1))
        x_pool = ctx.enter_context(tc.tile_pool(name="x_pool", bufs=BLOCKS))
        quant = ctx.enter_context(tc.tile_pool(name="quant", bufs=3))
        stats = ctx.enter_context(tc.tile_pool(name="stats", bufs=4))
        work = ctx.enter_context(tc.tile_pool(name="work", bufs=3))
        psum_t = ctx.enter_context(tc.psum_pool(name="psum_t", bufs=2))
        psum_q = ctx.enter_context(tc.psum_pool(name="psum_q", bufs=Q_TILES_IN_FLIGHT * BANKS))

        gain_row = const.tile([P, HEAD], BF16)
        nc.vector.memset(gain_row[:], 0.0)
        ones = const.tile([P, P], BF16)
        nc.vector.memset(ones[:], 1.0)
        x_tiles = []
        for block in range(BLOCKS):
            x_block = x_pool.tile([P, TILES_IN_BLOCK, K], BF16, name="x_block", tag="x_block")
            x_tiles.append(x_block)
        nc.sync.dma_start(out=x_tiles[0][:, 0, :], in_=x_blocks[0][:, 0, :])

        w_scales = const.tile([P, PASSES, HEADS * HEAD], U8, align_bytes=64)
        nc.vector.memset(w_scales[:].bitcast(I32), 0)
        scale_rows = wq_scales.bitcast(I32).rearrange("g q w -> q g w")
        for quadrant in range(4):
            nc.sync.dma_start(
                out=w_scales[32 * quadrant : 32 * quadrant + 4].bitcast(I32),
                in_=scale_rows[4 * quadrant : 4 * quadrant + 4],
            )
        w_words = const.tile([P, PASSES, 2 * HEADS * HEAD], U8, align_bytes=64)
        nc.sync.dma_start(out=w_words[:].bitcast(I32), in_=wq_words.bitcast(I32).rearrange("g p w -> p g w"))

        for n in range(1, TILES_IN_BLOCK):
            nc.sync.dma_start(out=x_tiles[0][:, n, :], in_=x_blocks[0][:, n, :])
        nc.sync.dma_start(out=x_tiles[1][:], in_=x_blocks[1])

        identity = const.tile([P, P], F32)
        make_identity(nc, identity[:])
        eps = const.tile([P, 1], F32)
        nc.vector.memset(eps[:], EPS)
        seq_tiles = SEQ_BLOCKS * TILES_IN_BLOCK
        trig = const.tile([P, 2, 2, seq_tiles, PAIRS], BF16)
        for plane, freqs in enumerate((freqs_cos, freqs_sin)):
            nc.scalar.dma_start(
                out=trig[:, 0, plane, :, :].rearrange("p (c n) j -> p c (n j)", n=TILES_IN_BLOCK),
                in_=freqs.rearrange("(c p n) j -> p c (n j)", p=P, n=TILES_IN_BLOCK),
            )
        nc.scalar.dma_start(out=gain_row[0:1, :], in_=q_norm_w.unsqueeze(0))
        warm = const.tile([P, 1], F32)
        nc.scalar.activation(out=warm[:], in_=eps[:], func=ACT.Abs_reciprocal_sqrt)

        table = const.tile([P, seq_tiles, PAIRS, 2, 2], F32)
        signed_gain = const.tile([P, PAIRS, 2, 2], F32)

        spread = {}

        def spread_gain():
            gain = psum_t.tile([P, PAIRS, 2], F32, name="flipped", tag="flipped")
            nc.tensor.matmul(out=gain[:].rearrange("p j i -> p (j i)"), lhsT=ones[:], rhs=gain_row[:], start=True, stop=True)
            spread["gain"] = gain

        def build_signed_gain():
            gain = spread["gain"]
            nc.vector.tensor_copy(out=signed_gain[:], in_=gain[:].unsqueeze(3).to_broadcast([P, PAIRS, 2, 2]))
            nc.vector.tensor_scalar_mul(out=signed_gain[:, :, 1, 0], in0=signed_gain[:, :, 1, 0], scalar1=-1.0)
            for e in range(2):
                nc.vector.tensor_copy(out=trig[:, 1, e, :, :], in_=trig[:, 0, 1 - e, :, :])

        def build_table(s):
            nc.vector.tensor_tensor(
                out=table[:, s, :, :, :],
                in0=trig[:, :, :, s, :].rearrange("p i e j -> p j i e"),
                in1=signed_gain[:],
                op=ALU.mult,
            )

        grouped_of = {}
        q_of = {}
        r_of = {}

        flipped_of = {}

        def transpose_tile(i):
            x_words = x_tiles[i // TILES_IN_BLOCK][:, i % TILES_IN_BLOCK, :].bitcast(F32)
            flipped = psum_t.tile([P, PASSES, 2, P], F32)
            for g in range(PASSES):
                for u in range(2):
                    nc.tensor.transpose(flipped[:, g, u, :], x_words[:, WORDS * g + u : WORDS * (g + 1) : 2], identity[:])
            flipped_of[i] = flipped

        def group_tile(i):
            flipped = flipped_of[i]
            grouped = quant.tile([P, PASSES * P * 4], BF16, align_bytes=64)
            nc.scalar.copy(
                out=grouped[:].bitcast(F32).rearrange("p (g r u) -> p g r u", g=PASSES, u=2),
                in_=flipped[:].rearrange("p g u r -> p g r u"),
            )
            grouped_of[i] = grouped

        def multiply_tile(i):
            x_codes = quant.tile([P, PASSES, P], U32, align_bytes=64)
            x_scales = quant.tile([P, PASSES, P], U8, align_bytes=64)
            nc.vector.quantize_mx(
                out=x_codes[:].rearrange("p g r -> p (g r)").bitcast(FP8X4),
                scales=x_scales[:].rearrange("p g r -> p (g r)"),
                in_=grouped_of[i][:],
            )
            banks = []
            for bank in range(BANKS):
                q = psum_q.tile([P, BANK], F32)
                for g in range(PASSES):
                    nc.tensor.matmul_mx(
                        out=q[:],
                        lhsT=x_codes[:, g, :].bitcast(FP8X4),
                        lhsT_scale=x_scales[:, g, :],
                        rhs=w_words[:, g, 2 * BANK * bank : 2 * BANK * (bank + 1)].bitcast(FP4X4),
                        rhs_scale=w_scales[:, g, BANK * bank : BANK * (bank + 1)],
                        start=(g == 0),
                        stop=(g == PASSES - 1),
                    )
                banks.append(q)
            q_of[i] = banks

        def norm_tile(i):
            sum_sq = stats.tile([P, HEADS], F32)
            r = stats.tile([P, HEADS], F32)
            for bank in range(BANKS):
                first, last = BANK_HEADS * bank, BANK_HEADS * (bank + 1)
                for h in range(first, last):
                    squares = work.tile([P, HEAD], F32)
                    nc.scalar.activation(
                        out=squares[:],
                        in_=q_of[i][bank][:, HEAD * (h - first) : HEAD * (h - first + 1)],
                        func=ACT.Square,
                        accum_out=sum_sq[:, h : h + 1],
                    )
                nc.scalar.activation(
                    out=r[:, first:last],
                    in_=sum_sq[:, first:last],
                    func=ACT.Abs_reciprocal_sqrt,
                    scale=1.0 / HEAD,
                    bias=eps[:, 0:1],
                )
            r_of[i] = r

        def rotate_tile(i):
            parts = work.tile([P, HEADS, PAIRS, 2, 2], F32)
            for h in range(HEADS):
                q_head = q_of[i][h // BANK_HEADS][:, HEAD * (h % BANK_HEADS) : HEAD * (h % BANK_HEADS + 1)]
                nc.vector.scalar_tensor_tensor(
                    out=parts[:, h, :, :, :].rearrange("p j i e -> p (j i) e"),
                    in0=q_head.unsqueeze(2).to_broadcast([P, HEAD, 2]),
                    scalar=r_of[i][:, h : h + 1],
                    in1=table[:, i % seq_tiles, :, :, :].rearrange("p j i e -> p (j i) e"),
                    op0=ALU.mult,
                    op1=ALU.mult,
                )
            result = work.tile([P, HEADS, PAIRS, 2], F32)
            if i < TILES - 1:
                nc.gpsimd.tensor_tensor(out=result[:], in0=parts[:, :, :, 0, :], in1=parts[:, :, :, 1, :], op=ALU.add)
                nc.sync.dma_start(
                    out=out_blocks[i // TILES_IN_BLOCK][:, i % TILES_IN_BLOCK, :],
                    in_=result[:].rearrange("p h j e -> p (h j e)"),
                )
            else:
                for bank in range(BANKS):
                    heads = slice(BANK_HEADS * bank, BANK_HEADS * (bank + 1))
                    nc.vector.tensor_tensor(
                        out=result[:, heads, :, :], in0=parts[:, heads, :, 0, :], in1=parts[:, heads, :, 1, :], op=ALU.add
                    )
                    nc.sync.dma_start(
                        out=out_blocks[i // TILES_IN_BLOCK][:, i % TILES_IN_BLOCK, BANK * bank : BANK * (bank + 1)],
                        in_=result[:, heads, :, :].rearrange("p h j e -> p (h j e)"),
                    )

        table_parts_in_step = {1: range(0, 4), 2: range(4, seq_tiles)}
        for step in range(TILES + 3):
            if (step + LOAD_AHEAD) % TILES_IN_BLOCK == 0 and 2 <= (step + LOAD_AHEAD) // TILES_IN_BLOCK < BLOCKS:
                block = (step + LOAD_AHEAD) // TILES_IN_BLOCK
                nc.sync.dma_start(out=x_tiles[block][:], in_=x_blocks[block])
            if step < TILES:
                transpose_tile(step)
            if step == 0:
                spread_gain()
            if 1 <= step <= TILES:
                multiply_tile(step - 1)
            if 2 <= step <= TILES + 1:
                norm_tile(step - 2)
            if step < TILES:
                group_tile(step)
            if step == 1:
                build_signed_gain()
            for s in table_parts_in_step.get(step, ()):
                build_table(s)
            if step == 2:
                rotate_tile(0)
            if step >= 4:
                rotate_tile(step - 3)
